import numpy as np
import ml_dtypes


def mxq(x, axis, fmt="e4m3"):
    dtype, down = {"e4m3": (ml_dtypes.float8_e4m3fn, 7), "e5m2": (ml_dtypes.float8_e5m2, 14)}[fmt]
    v = np.moveaxis(np.asarray(x, np.float32).astype(ml_dtypes.bfloat16).astype(np.float64), axis, -1)
    blocks = v.reshape(v.shape[:-1] + (-1, 32))
    amax = np.abs(blocks).max(-1, keepdims=True)
    byte = np.maximum(np.where(amax > 0, np.frexp(amax)[1] - 1 + 127, 0) - down, 1)
    scale = np.exp2(byte - 127.0)
    codes = (blocks / scale).astype(np.float32).astype(dtype).astype(np.float64)
    return np.moveaxis((codes * scale).reshape(v.shape), -1, axis)


WIDE = False


def mx_kscale(k):
    if not WIDE:
        return np.ones(k)
    levels = np.array([10, -10, 5, -5, 0])
    a = np.random.permutation(np.resize(levels, k // 512 * 4)).reshape(k // 512, 4)
    idx = np.arange(k)
    return np.exp2(a[idx // 512, idx % 128 // 32])


BF16 = ml_dtypes.bfloat16


def bf(x):
    return np.asarray(x, np.float32).astype(BF16)


def f64(x):
    return np.asarray(x).astype(np.float64)


B, S, I, Q = 4096, 3, 512, 512
LN_EPS = 1e-5


def setup_inputs():
    s = mx_kscale(I)
    return {"language_features": bf(np.random.standard_normal((B, I)) * s),
            "W": bf(np.random.standard_normal((S, I, Q)) / np.sqrt(I) / s[None, :, None]),
            "b": bf(np.random.standard_normal((S, Q)) * 0.2),
            "amplitude_weights": bf(np.random.standard_normal((S, Q))),
            "phase_weights": bf(np.random.standard_normal((S, Q))),
            "ln_gamma": bf(1.0 + 0.1 * np.random.standard_normal(Q)),
            "ln_beta": bf(0.1 * np.random.standard_normal(Q))}


def reference(language_features, W, b, amplitude_weights, phase_weights, ln_gamma, ln_beta):
    xq = mxq(f64(language_features), 1, "e4m3")
    wq = mxq(f64(W), 1, "e4m3")
    states = (xq @ wq).transpose(1, 0, 2) + f64(b)[None, :, :]
    a = f64(amplitude_weights)
    e = np.exp(a - a.max(axis=0, keepdims=True))
    amplitudes = e / e.sum(axis=0, keepdims=True)
    mix = amplitudes * np.cos(f64(phase_weights))
    sup = states * mix[None, :, :]
    mean = sup.mean(axis=-1, keepdims=True)
    var = sup.var(axis=-1, keepdims=True)
    return (sup - mean) * (1.0 / np.sqrt(var + LN_EPS)) * f64(ln_gamma) + f64(ln_beta)

@@ -1,0 +1,318 @@
+from contextlib import ExitStack
+
+import concourse.mybir as mybir
+from concourse.masks import make_identity
+
+F32 = mybir.dt.float32
+BF16 = mybir.dt.bfloat16
+U32 = mybir.dt.uint32
+U8 = mybir.dt.uint8
+FP8X4 = mybir.dt.float8_e4m3fn_x4
+ALU = mybir.AluOpType
+ACT = mybir.ActivationFunctionType
+
+P = 128
+ROWS = 4096
+K = 512
+Q = 512
+STATES = 3
+LN_EPS = 1e-5
+
+PACK = 4
+ROW_TILES = ROWS // P
+GROUP_TILES = 4
+GROUP_ROWS = GROUP_TILES * P
+GROUPS = ROW_TILES // GROUP_TILES
+Q_SLICES = Q // P
+UNITS = GROUPS * STATES
+TILES = UNITS * GROUP_TILES
+
+TWO_PI_HIGH = 6.28125
+TWO_PI_MID = 0.0019350051879882812
+TWO_PI_LOW = 3.019916050561733e-07
+ONE_OVER_TWO_PI = 0.15915494309189535
+ROUND_TO_WHOLE = 12582912.0
+
+FLOPS = 2 * ROWS * STATES * K * Q
+
+
+def tile_quantumsuperposition_t_kernel(
+    tc, language_features, W, b, amplitude_weights, phase_weights, ln_gamma, ln_beta, out
+):
+    nc = tc.nc
+    with ExitStack() as ctx:
+        consts = ctx.enter_context(tc.tile_pool(name="consts", bufs=1))
+        x_in = ctx.enter_context(tc.tile_pool(name="x_in", bufs=GROUPS))
+        x_mx = ctx.enter_context(tc.tile_pool(name="x_mx", bufs=2))
+        w_in = ctx.enter_context(tc.tile_pool(name="w_in", bufs=STATES))
+        sup_t_pool = ctx.enter_context(tc.tile_pool(name="sup_t", bufs=3))
+        y_pool = ctx.enter_context(tc.tile_pool(name="y", bufs=3 * GROUP_TILES))
+        stat_pool = ctx.enter_context(tc.tile_pool(name="stat", bufs=4))
+        psum_acc = ctx.enter_context(tc.psum_pool(name="psum_acc", bufs=3))
+        psum_sup = ctx.enter_context(tc.psum_pool(name="psum_sup", bufs=GROUP_TILES))
+        psum_x = ctx.enter_context(tc.psum_pool(name="psum_x", bufs=1))
+
+        x_view = language_features.rearrange("(p i) k -> p i k", i=ROW_TILES)
+        out_view = out.rearrange("(p i) s q -> p i s q", i=ROW_TILES)
+
+        w_rows = {}
+        x_rows = {}
+
+        def load_w(s):
+            rows = w_in.tile([P, PACK * Q], BF16, name="w_rows")
+            for u in range(2):
+                nc.sync.dma_start(
+                    out=rows[:, u * 2 * Q : (u + 1) * 2 * Q],
+                    in_=W[s, u * 2 * P : (u + 1) * 2 * P, :].rearrange("(p e) q -> p (e q)", e=2),
+                )
+            w_rows[s] = rows
+
+        def load_x(g):
+            rows = x_in.tile([P, GROUP_TILES * K], BF16, name="x_rows")
+            nc.sync.dma_start(
+                out=rows[:].rearrange("p (i k) -> p i k", i=GROUP_TILES),
+                in_=x_view[:, g * GROUP_TILES : (g + 1) * GROUP_TILES, :],
+            )
+            x_rows[g] = rows
+
+        load_w(0)
+        load_x(0)
+        gain_shift_rows = consts.tile([P, 2, Q], BF16)
+        nc.sync.dma_start(out=gain_shift_rows[:, 0, :], in_=ln_gamma.partition_broadcast(P))
+        nc.sync.dma_start(out=gain_shift_rows[:, 1, :], in_=ln_beta.partition_broadcast(P))
+        load_w(1)
+        load_w(2)
+        for g in range(1, GROUPS):
+            load_x(g)
+
+        vec_rows = consts.tile([P, P], BF16)
+        nc.vector.memset(vec_rows[:], 0.0)
+        vec_count = STATES * Q_SLICES
+        for n, vec in enumerate((b, amplitude_weights, phase_weights)):
+            nc.scalar.dma_start(
+                out=vec_rows[n * vec_count : (n + 1) * vec_count, :],
+                in_=vec.rearrange("s (j p) -> (s j) p", p=P),
+            )
+
+        ident = consts.tile([P, P], F32)
+        make_identity(nc, ident[:])
+        eps = consts.tile([P, 1], F32)
+        nc.vector.memset(eps[:], LN_EPS)
+
+        w_codes = consts.tile([P, STATES * Q], U32, align_bytes=64)
+        w_scales = consts.tile([P, STATES * Q], U8, align_bytes=64)
+
+        def quantise_w(s):
+            grouped = w_in.tile([P, Q * PACK], BF16, name="w_grouped", align_bytes=64)
+            nc.vector.tensor_copy(
+                out=grouped[:].rearrange("p (q t) -> p q t", t=PACK),
+                in_=w_rows[s][:].rearrange("p (t q) -> p q t", t=PACK),
+            )
+            nc.vector.quantize_mx(
+                out=w_codes[:, s * Q : (s + 1) * Q].bitcast(FP8X4),
+                scales=w_scales[:, s * Q : (s + 1) * Q],
+                in_=grouped[:],
+            )
+
+        x_codes = {}
+        x_scales = {}
+
+        def quantise_x(g):
+            words = x_rows[g][:].bitcast(F32)
+            grouped = x_mx.tile([P, GROUP_ROWS * PACK], BF16, name="x_grouped", align_bytes=64)
+            grouped_words = grouped[:].bitcast(F32).rearrange("p (c u) -> p c u", u=2)
+            for pair in range(GROUP_TILES // 2):
+                x_t = psum_x.tile([P, 2, 2 * P], F32, tag="small")
+                for ii in range(2):
+                    for u in range(2):
+                        first = ((2 * pair + ii) * 2 + u) * P
+                        nc.tensor.transpose(
+                            x_t[:, u, ii * P : (ii + 1) * P], words[:, first : first + P], ident[:]
+                        )
+                nc.scalar.copy(
+                    out=grouped_words[:, pair * 2 * P : (pair + 1) * 2 * P, :],
+                    in_=x_t[:].rearrange("p u c -> p c u"),
+                )
+            codes = x_mx.tile([P, GROUP_ROWS], U32, name="x_codes", align_bytes=64)
+            scales = x_mx.tile([P, GROUP_ROWS], U8, name="x_scales", align_bytes=64)
+            nc.vector.quantize_mx(out=codes[:].bitcast(FP8X4), scales=scales[:], in_=grouped[:])
+            x_codes[g] = codes
+            x_scales[g] = scales
+
+        quantise_w(0)
+        quantise_x(0)
+
+        vec_rows_f32 = consts.tile([P, P], F32)
+        nc.vector.tensor_copy(out=vec_rows_f32[:], in_=vec_rows[:])
+        vec_t = psum_x.tile([P, P], F32, tag="small")
+        nc.tensor.transpose(vec_t[:], vec_rows_f32[:], ident[:])
+        vecs = consts.tile([P, 3, STATES, Q_SLICES], F32)
+        nc.vector.tensor_copy(
+            out=vecs[:].rearrange("p n s j -> p (n s j)"), in_=vec_t[:, 0 : 3 * vec_count]
+        )
+        bias = vecs[:, 0, :, :]
+        amplitude = vecs[:, 1, :, :]
+        phase = vecs[:, 2, :, :]
+        per_state = [P, STATES, Q_SLICES]
+
+        top = consts.tile([P, Q_SLICES], F32)
+        nc.vector.tensor_max(out=top[:], in0=amplitude[:, 0, :], in1=amplitude[:, 1, :])
+        nc.vector.tensor_max(out=top[:], in0=top[:], in1=amplitude[:, 2, :])
+        shifted = consts.tile(per_state, F32)
+        nc.vector.tensor_tensor(
+            out=shifted[:], in0=amplitude, in1=top[:].unsqueeze(1).to_broadcast(per_state),
+            op=ALU.subtract,
+        )
+        expd = consts.tile(per_state, F32)
+        nc.scalar.activation(out=expd[:], in_=shifted[:], func=ACT.Exp)
+        total = consts.tile([P, Q_SLICES], F32)
+        nc.vector.tensor_add(out=total[:], in0=expd[:, 0, :], in1=expd[:, 1, :])
+        nc.vector.tensor_add(out=total[:], in0=total[:], in1=expd[:, 2, :])
+        one_over_total = consts.tile([P, Q_SLICES], F32)
+        nc.vector.reciprocal(out=one_over_total[:], in_=total[:])
+
+        turns = consts.tile(per_state, F32)
+        nc.vector.tensor_scalar(
+            out=turns[:], in0=phase, scalar1=ONE_OVER_TWO_PI, scalar2=ROUND_TO_WHOLE,
+            op0=ALU.mult, op1=ALU.add,
+        )
+        nc.vector.tensor_scalar_sub(out=turns[:], in0=turns[:], scalar1=ROUND_TO_WHOLE)
+        rest_a = consts.tile(per_state, F32)
+        nc.vector.scalar_tensor_tensor(
+            out=rest_a[:], in0=turns[:], scalar=-TWO_PI_HIGH, in1=phase, op0=ALU.mult, op1=ALU.add
+        )
+        rest_b = consts.tile(per_state, F32)
+        nc.vector.scalar_tensor_tensor(
+            out=rest_b[:], in0=turns[:], scalar=-TWO_PI_MID, in1=rest_a[:], op0=ALU.mult, op1=ALU.add
+        )
+        rest = consts.tile(per_state, F32)
+        nc.vector.scalar_tensor_tensor(
+            out=rest[:], in0=turns[:], scalar=-TWO_PI_LOW, in1=rest_b[:], op0=ALU.mult, op1=ALU.add
+        )
+        half_sin = consts.tile(per_state, F32)
+        nc.scalar.activation(out=half_sin[:], in_=rest[:], func=ACT.Sin, scale=0.5)
+        cosine = consts.tile(per_state, F32)
+        nc.vector.tensor_mul(out=cosine[:], in0=half_sin[:], in1=half_sin[:])
+        nc.vector.tensor_scalar(
+            out=cosine[:], in0=cosine[:], scalar1=-2.0, scalar2=1.0, op0=ALU.mult, op1=ALU.add
+        )
+
+        mix = consts.tile(per_state, F32)
+        nc.vector.tensor_mul(out=mix[:], in0=expd[:], in1=cosine[:])
+        nc.vector.tensor_mul(
+            out=mix[:], in0=mix[:], in1=one_over_total[:].unsqueeze(1).to_broadcast(per_state)
+        )
+        bias_mix = consts.tile(per_state, F32)
+        nc.vector.tensor_mul(out=bias_mix[:], in0=bias, in1=mix[:])
+
+        gain_shift = consts.tile([P, 2, Q], F32)
+        nc.gpsimd.tensor_copy(out=gain_shift[:], in_=gain_shift_rows[:])
+        gain = gain_shift[:, 0, :]
+        shift = gain_shift[:, 1, :]
+
+        quantise_w(1)
+        quantise_w(2)
+        quantise_x(1)
+
+        sup_t = {}
+        sup = {}
+        halves = {}
+        mean_var = {}
+        rstd = {}
+        y = {}
+
+        def unit_products(u):
+            g, s = divmod(u, STATES)
+            sup_t_u = sup_t_pool.tile([P, Q_SLICES, GROUP_ROWS], F32, name="sup_t")
+            for j in range(Q_SLICES):
+                cols = slice(s * Q + j * P, s * Q + (j + 1) * P)
+                acc = psum_acc.tile([P, GROUP_ROWS], F32, name="acc")
+                nc.tensor.matmul_mx(
+                    out=acc[:],
+                    lhsT=w_codes[:, cols].bitcast(FP8X4),
+                    lhsT_scale=w_scales[:, cols],
+                    rhs=x_codes[g][:].bitcast(FP8X4),
+                    rhs_scale=x_scales[g][:],
+                    start=True,
+                    stop=True,
+                )
+                nc.scalar.activation(
+                    out=sup_t_u[:, j, :], in_=acc[:], func=ACT.Identity,
+                    scale=mix[:, s, j : j + 1], bias=bias_mix[:, s, j : j + 1],
+                )
+            sup_t[u] = sup_t_u
+
+        def tile_transposes(t):
+            u, i = divmod(t, GROUP_TILES)
+            sup_tile = psum_sup.tile([P, Q], F32, name="sup")
+            for j in range(Q_SLICES):
+                nc.tensor.transpose(
+                    sup_tile[:, j * P : (j + 1) * P], sup_t[u][:, j, i * P : (i + 1) * P], ident[:]
+                )
+            sup[t] = sup_tile
+
+        def tile_halves(t):
+            halves_t = stat_pool.tile([P, 6], F32, name="halves")
+            nc.vector.bn_stats(out=halves_t[:], in_=sup[t][:])
+            halves[t] = halves_t
+
+        def tile_mean_var(t):
+            u, i = divmod(t, GROUP_TILES)
+            if i == 0:
+                mean_var_u = stat_pool.tile([P, GROUP_TILES, 2], F32, name="mean_var")
+                mean_var[u] = mean_var_u
+            nc.vector.bn_aggr(out=mean_var[u][:, i, :], in_=halves[t][:])
+
+        def tile_centre_and_gain(t):
+            u, i = divmod(t, GROUP_TILES)
+            y_t = y_pool.tile([P, Q], F32, name="y")
+            nc.vector.scalar_tensor_tensor(
+                out=y_t[:], in0=sup[t][:], scalar=mean_var[u][:, i, 0:1], in1=gain,
+                op0=ALU.subtract, op1=ALU.mult,
+            )
+            y[t] = y_t
+
+        def unit_rstd(u):
+            rstd_u = stat_pool.tile([P, GROUP_TILES], F32, name="rstd")
+            nc.scalar.activation(
+                out=rstd_u[:], in_=mean_var[u][:, :, 1], func=ACT.Abs_reciprocal_sqrt,
+                bias=eps[:, 0:1], scale=1.0,
+            )
+            rstd[u] = rstd_u
+
+        def tile_finish(t):
+            u, i = divmod(t, GROUP_TILES)
+            g, s = divmod(u, STATES)
+            nc.scalar.activation(out=y[t][:], in_=y[t][:], func=ACT.Copy, scale=rstd[u][:, i : i + 1])
+            nc.gpsimd.tensor_tensor(out=y[t][:], in0=y[t][:], in1=shift, op=ALU.add)
+            nc.sync.dma_start(out=out_view[:, g * GROUP_TILES + i, s, :], in_=y[t][:])
+
+        unit_products(0)
+        unit_products(1)
+        for t in range(GROUP_TILES):
+            tile_transposes(t)
+        tile_halves(0)
+        tile_mean_var(0)
+        for t in range(TILES):
+            u, i = divmod(t, GROUP_TILES)
+            if i == 0:
+                if u >= 1:
+                    unit_rstd(u - 1)
+                ahead = u + 2
+                if ahead < UNITS:
+                    unit_products(ahead)
+                    g_ahead, s_ahead = divmod(ahead, STATES)
+                    if s_ahead == 0 and g_ahead + 1 < GROUPS:
+                        quantise_x(g_ahead + 1)
+            if u >= 1:
+                tile_finish(t - GROUP_TILES)
+            if t + 1 < TILES:
+                tile_halves(t + 1)
+            tile_centre_and_gain(t)
+            if t + 1 < TILES:
+                tile_mean_var(t + 1)
+            if t + GROUP_TILES < TILES:
+                tile_transposes(t + GROUP_TILES)
+        unit_rstd(UNITS - 1)
+        for t in range(TILES - GROUP_TILES, TILES):
+            tile_finish(t)

@@ -51,6 +51,7 @@ def tile_quantumsuperposition_t_kernel(
         psum_acc = ctx.enter_context(tc.psum_pool(name="psum_acc", bufs=3))
         psum_sup = ctx.enter_context(tc.psum_pool(name="psum_sup", bufs=GROUP_TILES))
         psum_x = ctx.enter_context(tc.psum_pool(name="psum_x", bufs=1))
+        ctx.enter_context(tc.manual_schedule())
 
         x_view = language_features.rearrange("(p i) k -> p i k", i=ROW_TILES)
         out_view = out.rearrange("(p i) s q -> p i s q", i=ROW_TILES)

@@ -26,6 +26,7 @@ GROUPS = ROW_TILES // GROUP_TILES
 Q_SLICES = Q // P
 UNITS = GROUPS * STATES
 TILES = UNITS * GROUP_TILES
+LAG = GROUP_TILES - 1
 
 TWO_PI_HIGH = 6.28125
 TWO_PI_MID = 0.0019350051879882812
@@ -56,6 +57,19 @@ def tile_quantumsuperposition_t_kernel(
         x_view = language_features.rearrange("(p i) k -> p i k", i=ROW_TILES)
         out_view = out.rearrange("(p i) s q -> p i s q", i=ROW_TILES)
 
+        vec_rows = consts.tile([P, P], BF16)
+        nc.vector.memset(vec_rows[:], 0.0)
+        vec_count = STATES * Q_SLICES
+        for n, vec in enumerate((b, amplitude_weights, phase_weights)):
+            nc.scalar.dma_start(
+                out=vec_rows[n * vec_count : (n + 1) * vec_count, :],
+                in_=vec.rearrange("s (j p) -> (s j) p", p=P),
+            )
+        gain_shift_row = consts.tile([P, 2, Q], BF16)
+        nc.vector.memset(gain_shift_row[:], 0.0)
+        nc.scalar.dma_start(out=gain_shift_row[0:1, 0, :], in_=ln_gamma.unsqueeze(0))
+        nc.scalar.dma_start(out=gain_shift_row[0:1, 1, :], in_=ln_beta.unsqueeze(0))
+
         w_rows = {}
         x_rows = {}
 
@@ -76,27 +90,16 @@ def tile_quantumsuperposition_t_kernel(
             )
             x_rows[g] = rows
 
-        load_w(0)
         load_x(0)
-        gain_shift_rows = consts.tile([P, 2, Q], BF16)
-        nc.sync.dma_start(out=gain_shift_rows[:, 0, :], in_=ln_gamma.partition_broadcast(P))
-        nc.sync.dma_start(out=gain_shift_rows[:, 1, :], in_=ln_beta.partition_broadcast(P))
-        load_w(1)
-        load_w(2)
+        for s in range(STATES):
+            load_w(s)
         for g in range(1, GROUPS):
             load_x(g)
 
-        vec_rows = consts.tile([P, P], BF16)
-        nc.vector.memset(vec_rows[:], 0.0)
-        vec_count = STATES * Q_SLICES
-        for n, vec in enumerate((b, amplitude_weights, phase_weights)):
-            nc.scalar.dma_start(
-                out=vec_rows[n * vec_count : (n + 1) * vec_count, :],
-                in_=vec.rearrange("s (j p) -> (s j) p", p=P),
-            )
-
         ident = consts.tile([P, P], F32)
         make_identity(nc, ident[:])
+        ones = consts.tile([P, P], BF16)
+        nc.vector.memset(ones[:], 1.0)
         eps = consts.tile([P, 1], F32)
         nc.vector.memset(eps[:], LN_EPS)
 
@@ -115,33 +118,40 @@ def tile_quantumsuperposition_t_kernel(
                 in_=grouped[:],
             )
 
+        x_t = {}
+        x_grouped = {}
         x_codes = {}
         x_scales = {}
 
-        def quantise_x(g):
+        def x_transposes(g, pair):
             words = x_rows[g][:].bitcast(F32)
-            grouped = x_mx.tile([P, GROUP_ROWS * PACK], BF16, name="x_grouped", align_bytes=64)
-            grouped_words = grouped[:].bitcast(F32).rearrange("p (c u) -> p c u", u=2)
-            for pair in range(GROUP_TILES // 2):
-                x_t = psum_x.tile([P, 2, 2 * P], F32, tag="small")
-                for ii in range(2):
-                    for u in range(2):
-                        first = ((2 * pair + ii) * 2 + u) * P
-                        nc.tensor.transpose(
-                            x_t[:, u, ii * P : (ii + 1) * P], words[:, first : first + P], ident[:]
-                        )
-                nc.scalar.copy(
-                    out=grouped_words[:, pair * 2 * P : (pair + 1) * 2 * P, :],
-                    in_=x_t[:].rearrange("p u c -> p c u"),
-                )
+            x_t_pair = psum_x.tile([P, 2, 2 * P], F32, tag="small")
+            for ii in range(2):
+                for u in range(2):
+                    first = ((2 * pair + ii) * 2 + u) * P
+                    nc.tensor.transpose(
+                        x_t_pair[:, u, ii * P : (ii + 1) * P], words[:, first : first + P], ident[:]
+                    )
+            x_t[g, pair] = x_t_pair
+
+        def x_regroup(g, pair):
+            if pair == 0:
+                grouped = x_mx.tile([P, GROUP_ROWS * PACK], BF16, name="x_grouped", align_bytes=64)
+                x_grouped[g] = grouped
+            grouped_words = x_grouped[g][:].bitcast(F32).rearrange("p (c u) -> p c u", u=2)
+            nc.scalar.copy(
+                out=grouped_words[:, pair * 2 * P : (pair + 1) * 2 * P, :],
+                in_=x_t[g, pair][:].rearrange("p u c -> p c u"),
+            )
+
+        def x_quantise(g):
             codes = x_mx.tile([P, GROUP_ROWS], U32, name="x_codes", align_bytes=64)
             scales = x_mx.tile([P, GROUP_ROWS], U8, name="x_scales", align_bytes=64)
-            nc.vector.quantize_mx(out=codes[:].bitcast(FP8X4), scales=scales[:], in_=grouped[:])
+            nc.vector.quantize_mx(
+                out=codes[:].bitcast(FP8X4), scales=scales[:], in_=x_grouped[g][:]
+            )
             x_codes[g] = codes
             x_scales[g] = scales
-
-        quantise_w(0)
-        quantise_x(0)
 
         vec_rows_f32 = consts.tile([P, P], F32)
         nc.vector.tensor_copy(out=vec_rows_f32[:], in_=vec_rows[:])
@@ -166,11 +176,6 @@ def tile_quantumsuperposition_t_kernel(
         )
         expd = consts.tile(per_state, F32)
         nc.scalar.activation(out=expd[:], in_=shifted[:], func=ACT.Exp)
-        total = consts.tile([P, Q_SLICES], F32)
-        nc.vector.tensor_add(out=total[:], in0=expd[:, 0, :], in1=expd[:, 1, :])
-        nc.vector.tensor_add(out=total[:], in0=total[:], in1=expd[:, 2, :])
-        one_over_total = consts.tile([P, Q_SLICES], F32)
-        nc.vector.reciprocal(out=one_over_total[:], in_=total[:])
 
         turns = consts.tile(per_state, F32)
         nc.vector.tensor_scalar(
@@ -192,12 +197,32 @@ def tile_quantumsuperposition_t_kernel(
         )
         half_sin = consts.tile(per_state, F32)
         nc.scalar.activation(out=half_sin[:], in_=rest[:], func=ACT.Sin, scale=0.5)
+
+        gain_shift = consts.tile([P, 2, Q], F32)
+        for n in range(2):
+            spread = psum_acc.tile([P, Q], F32, name="acc")
+            nc.tensor.matmul(
+                out=spread[:], lhsT=ones[:], rhs=gain_shift_row[:, n, :], start=True, stop=True
+            )
+            nc.vector.tensor_copy(out=gain_shift[:, n, :], in_=spread[:])
+        gain = gain_shift[:, 0, :]
+        shift = gain_shift[:, 1, :]
+
+        for pair in range(2):
+            x_transposes(0, pair)
+            x_regroup(0, pair)
+        quantise_w(0)
+
+        total = consts.tile([P, Q_SLICES], F32)
+        nc.vector.tensor_add(out=total[:], in0=expd[:, 0, :], in1=expd[:, 1, :])
+        nc.vector.tensor_add(out=total[:], in0=total[:], in1=expd[:, 2, :])
+        one_over_total = consts.tile([P, Q_SLICES], F32)
+        nc.vector.reciprocal(out=one_over_total[:], in_=total[:])
         cosine = consts.tile(per_state, F32)
         nc.vector.tensor_mul(out=cosine[:], in0=half_sin[:], in1=half_sin[:])
         nc.vector.tensor_scalar(
             out=cosine[:], in0=cosine[:], scalar1=-2.0, scalar2=1.0, op0=ALU.mult, op1=ALU.add
         )
-
         mix = consts.tile(per_state, F32)
         nc.vector.tensor_mul(out=mix[:], in0=expd[:], in1=cosine[:])
         nc.vector.tensor_mul(
@@ -206,15 +231,16 @@ def tile_quantumsuperposition_t_kernel(
         bias_mix = consts.tile(per_state, F32)
         nc.vector.tensor_mul(out=bias_mix[:], in0=bias, in1=mix[:])
 
-        gain_shift = consts.tile([P, 2, Q], F32)
-        nc.gpsimd.tensor_copy(out=gain_shift[:], in_=gain_shift_rows[:])
-        gain = gain_shift[:, 0, :]
-        shift = gain_shift[:, 1, :]
-
+        x_quantise(0)
         quantise_w(1)
         quantise_w(2)
-        quantise_x(1)
 
+        table_warmer = consts.tile([P, 1], F32)
+        nc.scalar.activation(
+            out=table_warmer[:], in_=eps[:], func=ACT.Abs_reciprocal_sqrt, bias=eps[:, 0:1], scale=1.0
+        )
+
+        acc = {}
         sup_t = {}
         sup = {}
         halves = {}
@@ -222,26 +248,30 @@ def tile_quantumsuperposition_t_kernel(
         rstd = {}
         y = {}
 
-        def unit_products(u):
+        def slice_products(u, j):
             g, s = divmod(u, STATES)
-            sup_t_u = sup_t_pool.tile([P, Q_SLICES, GROUP_ROWS], F32, name="sup_t")
-            for j in range(Q_SLICES):
-                cols = slice(s * Q + j * P, s * Q + (j + 1) * P)
-                acc = psum_acc.tile([P, GROUP_ROWS], F32, name="acc")
-                nc.tensor.matmul_mx(
-                    out=acc[:],
-                    lhsT=w_codes[:, cols].bitcast(FP8X4),
-                    lhsT_scale=w_scales[:, cols],
-                    rhs=x_codes[g][:].bitcast(FP8X4),
-                    rhs_scale=x_scales[g][:],
-                    start=True,
-                    stop=True,
-                )
-                nc.scalar.activation(
-                    out=sup_t_u[:, j, :], in_=acc[:], func=ACT.Identity,
-                    scale=mix[:, s, j : j + 1], bias=bias_mix[:, s, j : j + 1],
-                )
-            sup_t[u] = sup_t_u
+            cols = slice(s * Q + j * P, s * Q + (j + 1) * P)
+            acc_j = psum_acc.tile([P, GROUP_ROWS], F32, name="acc")
+            nc.tensor.matmul_mx(
+                out=acc_j[:],
+                lhsT=w_codes[:, cols].bitcast(FP8X4),
+                lhsT_scale=w_scales[:, cols],
+                rhs=x_codes[g][:].bitcast(FP8X4),
+                rhs_scale=x_scales[g][:],
+                start=True,
+                stop=True,
+            )
+            acc[u, j] = acc_j
+
+        def slice_mix(u, j):
+            s = u % STATES
+            if j == 0:
+                sup_t_u = sup_t_pool.tile([P, Q_SLICES, GROUP_ROWS], F32, name="sup_t")
+                sup_t[u] = sup_t_u
+            nc.scalar.activation(
+                out=sup_t[u][:, j, :], in_=acc[u, j][:], func=ACT.Identity,
+                scale=mix[:, s, j : j + 1], bias=bias_mix[:, s, j : j + 1],
+            )
 
         def tile_transposes(t):
             u, i = divmod(t, GROUP_TILES)
@@ -284,36 +314,43 @@ def tile_quantumsuperposition_t_kernel(
         def tile_finish(t):
             u, i = divmod(t, GROUP_TILES)
             g, s = divmod(u, STATES)
-            nc.scalar.activation(out=y[t][:], in_=y[t][:], func=ACT.Copy, scale=rstd[u][:, i : i + 1])
-            nc.gpsimd.tensor_tensor(out=y[t][:], in0=y[t][:], in1=shift, op=ALU.add)
+            if u < UNITS - 1:
+                nc.scalar.activation(
+                    out=y[t][:], in_=y[t][:], func=ACT.Copy, scale=rstd[u][:, i : i + 1]
+                )
+                nc.gpsimd.tensor_tensor(out=y[t][:], in0=y[t][:], in1=shift, op=ALU.add)
+            else:
+                nc.vector.scalar_tensor_tensor(
+                    out=y[t][:], in0=y[t][:], scalar=rstd[u][:, i : i + 1], in1=shift,
+                    op0=ALU.mult, op1=ALU.add,
+                )
             nc.sync.dma_start(out=out_view[:, g * GROUP_TILES + i, s, :], in_=y[t][:])
 
-        unit_products(0)
-        unit_products(1)
-        for t in range(GROUP_TILES):
-            tile_transposes(t)
-        tile_halves(0)
-        tile_mean_var(0)
-        for t in range(TILES):
+        for t in range(-2 * GROUP_TILES, TILES + LAG):
             u, i = divmod(t, GROUP_TILES)
-            if i == 0:
-                if u >= 1:
-                    unit_rstd(u - 1)
-                ahead = u + 2
-                if ahead < UNITS:
-                    unit_products(ahead)
-                    g_ahead, s_ahead = divmod(ahead, STATES)
-                    if s_ahead == 0 and g_ahead + 1 < GROUPS:
-                        quantise_x(g_ahead + 1)
-            if u >= 1:
-                tile_finish(t - GROUP_TILES)
-            if t + 1 < TILES:
+            ahead = u + 2
+            if i == LAG and 0 <= u < UNITS:
+                unit_rstd(u)
+            if ahead < UNITS:
+                slice_products(ahead, i)
+            g_next = ahead // STATES + 1
+            pair = ahead % STATES - 1
+            if g_next < GROUPS and pair >= 0:
+                if i == 0:
+                    x_transposes(g_next, pair)
+                if i == 1:
+                    x_regroup(g_next, pair)
+                if i == 3 and pair == 1:
+                    x_quantise(g_next)
+            if ahead < UNITS:
+                slice_mix(ahead, i)
+            if 0 <= t + 1 < TILES:
                 tile_halves(t + 1)
-            tile_centre_and_gain(t)
-            if t + 1 < TILES:
+            if 0 <= t < TILES:
+                tile_centre_and_gain(t)
+            if 0 <= t + 1 < TILES:
                 tile_mean_var(t + 1)
-            if t + GROUP_TILES < TILES:
+            if 0 <= t + GROUP_TILES < TILES:
                 tile_transposes(t + GROUP_TILES)
-        unit_rstd(UNITS - 1)
-        for t in range(TILES - GROUP_TILES, TILES):
-            tile_finish(t)
+            if 0 <= t - LAG:
+                tile_finish(t - LAG)

@@ -49,9 +49,8 @@ def tile_quantumsuperposition_t_kernel(
         sup_t_pool = ctx.enter_context(tc.tile_pool(name="sup_t", bufs=3))
         y_pool = ctx.enter_context(tc.tile_pool(name="y", bufs=3 * GROUP_TILES))
         stat_pool = ctx.enter_context(tc.tile_pool(name="stat", bufs=4))
-        psum_acc = ctx.enter_context(tc.psum_pool(name="psum_acc", bufs=3))
+        psum_acc = ctx.enter_context(tc.psum_pool(name="psum_acc", bufs=Q_SLICES))
         psum_sup = ctx.enter_context(tc.psum_pool(name="psum_sup", bufs=GROUP_TILES))
-        psum_x = ctx.enter_context(tc.psum_pool(name="psum_x", bufs=1))
         ctx.enter_context(tc.manual_schedule())
 
         x_view = language_features.rearrange("(p i) k -> p i k", i=ROW_TILES)
@@ -125,7 +124,7 @@ def tile_quantumsuperposition_t_kernel(
 
         def x_transposes(g, pair):
             words = x_rows[g][:].bitcast(F32)
-            x_t_pair = psum_x.tile([P, 2, 2 * P], F32, tag="small")
+            x_t_pair = psum_acc.tile([P, 2, 2 * P], F32, tag="acc")
             for ii in range(2):
                 for u in range(2):
                     first = ((2 * pair + ii) * 2 + u) * P
@@ -155,7 +154,7 @@ def tile_quantumsuperposition_t_kernel(
 
         vec_rows_f32 = consts.tile([P, P], F32)
         nc.vector.tensor_copy(out=vec_rows_f32[:], in_=vec_rows[:])
-        vec_t = psum_x.tile([P, P], F32, tag="small")
+        vec_t = psum_acc.tile([P, P], F32, tag="acc")
         nc.tensor.transpose(vec_t[:], vec_rows_f32[:], ident[:])
         vecs = consts.tile([P, 3, STATES, Q_SLICES], F32)
         nc.vector.tensor_copy(
@@ -331,14 +330,15 @@ def tile_quantumsuperposition_t_kernel(
             ahead = u + 2
             if i == LAG and 0 <= u < UNITS:
                 unit_rstd(u)
-            if ahead < UNITS:
-                slice_products(ahead, i)
+            if i == 0 and ahead < UNITS:
+                for j in range(Q_SLICES):
+                    slice_products(ahead, j)
             g_next = ahead // STATES + 1
             pair = ahead % STATES - 1
             if g_next < GROUPS and pair >= 0:
-                if i == 0:
-                    x_transposes(g_next, pair)
                 if i == 1:
+                    x_transposes(g_next, pair)
+                if i == 2:
                     x_regroup(g_next, pair)
                 if i == 3 and pair == 1:
                     x_quantise(g_next)

@@ -26,6 +26,7 @@ GROUPS = ROW_TILES // GROUP_TILES
 Q_SLICES = Q // P
 UNITS = GROUPS * STATES
 TILES = UNITS * GROUP_TILES
+ISSUES_PER_PASS = 2
 LAG = GROUP_TILES - 1
 
 TWO_PI_HIGH = 6.28125
@@ -49,8 +50,9 @@ def tile_quantumsuperposition_t_kernel(
         sup_t_pool = ctx.enter_context(tc.tile_pool(name="sup_t", bufs=3))
         y_pool = ctx.enter_context(tc.tile_pool(name="y", bufs=3 * GROUP_TILES))
         stat_pool = ctx.enter_context(tc.tile_pool(name="stat", bufs=4))
-        psum_acc = ctx.enter_context(tc.psum_pool(name="psum_acc", bufs=Q_SLICES))
+        psum_acc = ctx.enter_context(tc.psum_pool(name="psum_acc", bufs=3))
         psum_sup = ctx.enter_context(tc.psum_pool(name="psum_sup", bufs=GROUP_TILES))
+        psum_x = ctx.enter_context(tc.psum_pool(name="psum_x", bufs=1))
         ctx.enter_context(tc.manual_schedule())
 
         x_view = language_features.rearrange("(p i) k -> p i k", i=ROW_TILES)
@@ -124,7 +126,7 @@ def tile_quantumsuperposition_t_kernel(
 
         def x_transposes(g, pair):
             words = x_rows[g][:].bitcast(F32)
-            x_t_pair = psum_acc.tile([P, 2, 2 * P], F32, tag="acc")
+            x_t_pair = psum_x.tile([P, 2, 2 * P], F32, tag="small")
             for ii in range(2):
                 for u in range(2):
                     first = ((2 * pair + ii) * 2 + u) * P
@@ -154,7 +156,7 @@ def tile_quantumsuperposition_t_kernel(
 
         vec_rows_f32 = consts.tile([P, P], F32)
         nc.vector.tensor_copy(out=vec_rows_f32[:], in_=vec_rows[:])
-        vec_t = psum_acc.tile([P, P], F32, tag="acc")
+        vec_t = psum_x.tile([P, P], F32, tag="small")
         nc.tensor.transpose(vec_t[:], vec_rows_f32[:], ident[:])
         vecs = consts.tile([P, 3, STATES, Q_SLICES], F32)
         nc.vector.tensor_copy(
@@ -251,15 +253,16 @@ def tile_quantumsuperposition_t_kernel(
             g, s = divmod(u, STATES)
             cols = slice(s * Q + j * P, s * Q + (j + 1) * P)
             acc_j = psum_acc.tile([P, GROUP_ROWS], F32, name="acc")
-            nc.tensor.matmul_mx(
-                out=acc_j[:],
-                lhsT=w_codes[:, cols].bitcast(FP8X4),
-                lhsT_scale=w_scales[:, cols],
-                rhs=x_codes[g][:].bitcast(FP8X4),
-                rhs_scale=x_scales[g][:],
-                start=True,
-                stop=True,
-            )
+            for issue in range(ISSUES_PER_PASS):
+                nc.tensor.matmul_mx(
+                    out=acc_j[:],
+                    lhsT=w_codes[:, cols].bitcast(FP8X4),
+                    lhsT_scale=w_scales[:, cols],
+                    rhs=x_codes[g][:].bitcast(FP8X4),
+                    rhs_scale=x_scales[g][:],
+                    start=True,
+                    stop=True,
+                )
             acc[u, j] = acc_j
 
         def slice_mix(u, j):
@@ -330,15 +333,14 @@ def tile_quantumsuperposition_t_kernel(
             ahead = u + 2
             if i == LAG and 0 <= u < UNITS:
                 unit_rstd(u)
-            if i == 0 and ahead < UNITS:
-                for j in range(Q_SLICES):
-                    slice_products(ahead, j)
+            if ahead < UNITS:
+                slice_products(ahead, i)
             g_next = ahead // STATES + 1
             pair = ahead % STATES - 1
             if g_next < GROUPS and pair >= 0:
-                if i == 1:
+                if i == 0:
                     x_transposes(g_next, pair)
-                if i == 2:
+                if i == 1:
                     x_regroup(g_next, pair)
                 if i == 3 and pair == 1:
                     x_quantise(g_next)

from contextlib import ExitStack

import concourse.mybir as mybir
from concourse.masks import make_identity

F32 = mybir.dt.float32
BF16 = mybir.dt.bfloat16
U32 = mybir.dt.uint32
U8 = mybir.dt.uint8
FP8X4 = mybir.dt.float8_e4m3fn_x4
ALU = mybir.AluOpType
ACT = mybir.ActivationFunctionType

P = 128
ROWS = 4096
K = 512
Q = 512
STATES = 3
LN_EPS = 1e-5

PACK = 4
ROW_TILES = ROWS // P
GROUP_TILES = 4
GROUP_ROWS = GROUP_TILES * P
GROUPS = ROW_TILES // GROUP_TILES
Q_SLICES = Q // P
UNITS = GROUPS * STATES
TILES = UNITS * GROUP_TILES
ISSUES_PER_PASS = 2
LAG = GROUP_TILES - 1

TWO_PI_HIGH = 6.28125
TWO_PI_MID = 0.0019350051879882812
TWO_PI_LOW = 3.019916050561733e-07
ONE_OVER_TWO_PI = 0.15915494309189535
ROUND_TO_WHOLE = 12582912.0

FLOPS = 2 * ROWS * STATES * K * Q


def tile_quantumsuperposition_t_kernel(
    tc, language_features, W, b, amplitude_weights, phase_weights, ln_gamma, ln_beta, out
):
    nc = tc.nc
    with ExitStack() as ctx:
        consts = ctx.enter_context(tc.tile_pool(name="consts", bufs=1))
        x_in = ctx.enter_context(tc.tile_pool(name="x_in", bufs=GROUPS))
        x_mx = ctx.enter_context(tc.tile_pool(name="x_mx", bufs=2))
        w_in = ctx.enter_context(tc.tile_pool(name="w_in", bufs=STATES))
        sup_t_pool = ctx.enter_context(tc.tile_pool(name="sup_t", bufs=3))
        y_pool = ctx.enter_context(tc.tile_pool(name="y", bufs=3 * GROUP_TILES))
        stat_pool = ctx.enter_context(tc.tile_pool(name="stat", bufs=4))
        psum_acc = ctx.enter_context(tc.psum_pool(name="psum_acc", bufs=3))
        psum_sup = ctx.enter_context(tc.psum_pool(name="psum_sup", bufs=GROUP_TILES))
        psum_x = ctx.enter_context(tc.psum_pool(name="psum_x", bufs=1))
        ctx.enter_context(tc.manual_schedule())

        x_view = language_features.rearrange("(p i) k -> p i k", i=ROW_TILES)
        out_view = out.rearrange("(p i) s q -> p i s q", i=ROW_TILES)

        vec_rows = consts.tile([P, P], BF16)
        nc.vector.memset(vec_rows[:], 0.0)
        vec_count = STATES * Q_SLICES
        for n, vec in enumerate((b, amplitude_weights, phase_weights)):
            nc.scalar.dma_start(
                out=vec_rows[n * vec_count : (n + 1) * vec_count, :],
                in_=vec.rearrange("s (j p) -> (s j) p", p=P),
            )
        gain_shift_row = consts.tile([P, 2, Q], BF16)
        nc.vector.memset(gain_shift_row[:], 0.0)
        nc.scalar.dma_start(out=gain_shift_row[0:1, 0, :], in_=ln_gamma.unsqueeze(0))
        nc.scalar.dma_start(out=gain_shift_row[0:1, 1, :], in_=ln_beta.unsqueeze(0))

        w_rows = {}
        x_rows = {}

        def load_w(s):
            rows = w_in.tile([P, PACK * Q], BF16, name="w_rows")
            for u in range(2):
                nc.sync.dma_start(
                    out=rows[:, u * 2 * Q : (u + 1) * 2 * Q],
                    in_=W[s, u * 2 * P : (u + 1) * 2 * P, :].rearrange("(p e) q -> p (e q)", e=2),
                )
            w_rows[s] = rows

        def load_x(g):
            rows = x_in.tile([P, GROUP_TILES * K], BF16, name="x_rows")
            nc.sync.dma_start(
                out=rows[:].rearrange("p (i k) -> p i k", i=GROUP_TILES),
                in_=x_view[:, g * GROUP_TILES : (g + 1) * GROUP_TILES, :],
            )
            x_rows[g] = rows

        load_x(0)
        for s in range(STATES):
            load_w(s)
        for g in range(1, GROUPS):
            load_x(g)

        ident = consts.tile([P, P], F32)
        make_identity(nc, ident[:])
        ones = consts.tile([P, P], BF16)
        nc.vector.memset(ones[:], 1.0)
        eps = consts.tile([P, 1], F32)
        nc.vector.memset(eps[:], LN_EPS)

        w_codes = consts.tile([P, STATES * Q], U32, align_bytes=64)
        w_scales = consts.tile([P, STATES * Q], U8, align_bytes=64)

        def quantise_w(s):
            grouped = w_in.tile([P, Q * PACK], BF16, name="w_grouped", align_bytes=64)
            nc.vector.tensor_copy(
                out=grouped[:].rearrange("p (q t) -> p q t", t=PACK),
                in_=w_rows[s][:].rearrange("p (t q) -> p q t", t=PACK),
            )
            nc.vector.quantize_mx(
                out=w_codes[:, s * Q : (s + 1) * Q].bitcast(FP8X4),
                scales=w_scales[:, s * Q : (s + 1) * Q],
                in_=grouped[:],
            )

        x_t = {}
        x_grouped = {}
        x_codes = {}
        x_scales = {}

        def x_transposes(g, pair):
            words = x_rows[g][:].bitcast(F32)
            x_t_pair = psum_x.tile([P, 2, 2 * P], F32, tag="small")
            for ii in range(2):
                for u in range(2):
                    first = ((2 * pair + ii) * 2 + u) * P
                    nc.tensor.transpose(
                        x_t_pair[:, u, ii * P : (ii + 1) * P], words[:, first : first + P], ident[:]
                    )
            x_t[g, pair] = x_t_pair

        def x_regroup(g, pair):
            if pair == 0:
                grouped = x_mx.tile([P, GROUP_ROWS * PACK], BF16, name="x_grouped", align_bytes=64)
                x_grouped[g] = grouped
            grouped_words = x_grouped[g][:].bitcast(F32).rearrange("p (c u) -> p c u", u=2)
            nc.scalar.copy(
                out=grouped_words[:, pair * 2 * P : (pair + 1) * 2 * P, :],
                in_=x_t[g, pair][:].rearrange("p u c -> p c u"),
            )

        def x_quantise(g):
            codes = x_mx.tile([P, GROUP_ROWS], U32, name="x_codes", align_bytes=64)
            scales = x_mx.tile([P, GROUP_ROWS], U8, name="x_scales", align_bytes=64)
            nc.vector.quantize_mx(
                out=codes[:].bitcast(FP8X4), scales=scales[:], in_=x_grouped[g][:]
            )
            x_codes[g] = codes
            x_scales[g] = scales

        vec_rows_f32 = consts.tile([P, P], F32)
        nc.vector.tensor_copy(out=vec_rows_f32[:], in_=vec_rows[:])
        vec_t = psum_x.tile([P, P], F32, tag="small")
        nc.tensor.transpose(vec_t[:], vec_rows_f32[:], ident[:])
        vecs = consts.tile([P, 3, STATES, Q_SLICES], F32)
        nc.vector.tensor_copy(
            out=vecs[:].rearrange("p n s j -> p (n s j)"), in_=vec_t[:, 0 : 3 * vec_count]
        )
        bias = vecs[:, 0, :, :]
        amplitude = vecs[:, 1, :, :]
        phase = vecs[:, 2, :, :]
        per_state = [P, STATES, Q_SLICES]

        top = consts.tile([P, Q_SLICES], F32)
        nc.vector.tensor_max(out=top[:], in0=amplitude[:, 0, :], in1=amplitude[:, 1, :])
        nc.vector.tensor_max(out=top[:], in0=top[:], in1=amplitude[:, 2, :])
        shifted = consts.tile(per_state, F32)
        nc.vector.tensor_tensor(
            out=shifted[:], in0=amplitude, in1=top[:].unsqueeze(1).to_broadcast(per_state),
            op=ALU.subtract,
        )
        expd = consts.tile(per_state, F32)
        nc.scalar.activation(out=expd[:], in_=shifted[:], func=ACT.Exp)

        turns = consts.tile(per_state, F32)
        nc.vector.tensor_scalar(
            out=turns[:], in0=phase, scalar1=ONE_OVER_TWO_PI, scalar2=ROUND_TO_WHOLE,
            op0=ALU.mult, op1=ALU.add,
        )
        nc.vector.tensor_scalar_sub(out=turns[:], in0=turns[:], scalar1=ROUND_TO_WHOLE)
        rest_a = consts.tile(per_state, F32)
        nc.vector.scalar_tensor_tensor(
            out=rest_a[:], in0=turns[:], scalar=-TWO_PI_HIGH, in1=phase, op0=ALU.mult, op1=ALU.add
        )
        rest_b = consts.tile(per_state, F32)
        nc.vector.scalar_tensor_tensor(
            out=rest_b[:], in0=turns[:], scalar=-TWO_PI_MID, in1=rest_a[:], op0=ALU.mult, op1=ALU.add
        )
        rest = consts.tile(per_state, F32)
        nc.vector.scalar_tensor_tensor(
            out=rest[:], in0=turns[:], scalar=-TWO_PI_LOW, in1=rest_b[:], op0=ALU.mult, op1=ALU.add
        )
        half_sin = consts.tile(per_state, F32)
        nc.scalar.activation(out=half_sin[:], in_=rest[:], func=ACT.Sin, scale=0.5)

        gain_shift = consts.tile([P, 2, Q], F32)
        for n in range(2):
            spread = psum_acc.tile([P, Q], F32, name="acc")
            nc.tensor.matmul(
                out=spread[:], lhsT=ones[:], rhs=gain_shift_row[:, n, :], start=True, stop=True
            )
            nc.vector.tensor_copy(out=gain_shift[:, n, :], in_=spread[:])
        gain = gain_shift[:, 0, :]
        shift = gain_shift[:, 1, :]

        for pair in range(2):
            x_transposes(0, pair)
            x_regroup(0, pair)
        quantise_w(0)

        total = consts.tile([P, Q_SLICES], F32)
        nc.vector.tensor_add(out=total[:], in0=expd[:, 0, :], in1=expd[:, 1, :])
        nc.vector.tensor_add(out=total[:], in0=total[:], in1=expd[:, 2, :])
        one_over_total = consts.tile([P, Q_SLICES], F32)
        nc.vector.reciprocal(out=one_over_total[:], in_=total[:])
        cosine = consts.tile(per_state, F32)
        nc.vector.tensor_mul(out=cosine[:], in0=half_sin[:], in1=half_sin[:])
        nc.vector.tensor_scalar(
            out=cosine[:], in0=cosine[:], scalar1=-2.0, scalar2=1.0, op0=ALU.mult, op1=ALU.add
        )
        mix = consts.tile(per_state, F32)
        nc.vector.tensor_mul(out=mix[:], in0=expd[:], in1=cosine[:])
        nc.vector.tensor_mul(
            out=mix[:], in0=mix[:], in1=one_over_total[:].unsqueeze(1).to_broadcast(per_state)
        )
        bias_mix = consts.tile(per_state, F32)
        nc.vector.tensor_mul(out=bias_mix[:], in0=bias, in1=mix[:])

        x_quantise(0)
        quantise_w(1)
        quantise_w(2)

        table_warmer = consts.tile([P, 1], F32)
        nc.scalar.activation(
            out=table_warmer[:], in_=eps[:], func=ACT.Abs_reciprocal_sqrt, bias=eps[:, 0:1], scale=1.0
        )

        acc = {}
        sup_t = {}
        sup = {}
        halves = {}
        mean_var = {}
        rstd = {}
        y = {}

        def slice_products(u, j):
            g, s = divmod(u, STATES)
            cols = slice(s * Q + j * P, s * Q + (j + 1) * P)
            acc_j = psum_acc.tile([P, GROUP_ROWS], F32, name="acc")
            for issue in range(ISSUES_PER_PASS):
                nc.tensor.matmul_mx(
                    out=acc_j[:],
                    lhsT=w_codes[:, cols].bitcast(FP8X4),
                    lhsT_scale=w_scales[:, cols],
                    rhs=x_codes[g][:].bitcast(FP8X4),
                    rhs_scale=x_scales[g][:],
                    start=True,
                    stop=True,
                )
            acc[u, j] = acc_j

        def slice_mix(u, j):
            s = u % STATES
            if j == 0:
                sup_t_u = sup_t_pool.tile([P, Q_SLICES, GROUP_ROWS], F32, name="sup_t")
                sup_t[u] = sup_t_u
            nc.scalar.activation(
                out=sup_t[u][:, j, :], in_=acc[u, j][:], func=ACT.Identity,
                scale=mix[:, s, j : j + 1], bias=bias_mix[:, s, j : j + 1],
            )

        def tile_transposes(t):
            u, i = divmod(t, GROUP_TILES)
            sup_tile = psum_sup.tile([P, Q], F32, name="sup")
            for j in range(Q_SLICES):
                nc.tensor.transpose(
                    sup_tile[:, j * P : (j + 1) * P], sup_t[u][:, j, i * P : (i + 1) * P], ident[:]
                )
            sup[t] = sup_tile

        def tile_halves(t):
            halves_t = stat_pool.tile([P, 6], F32, name="halves")
            nc.vector.bn_stats(out=halves_t[:], in_=sup[t][:])
            halves[t] = halves_t

        def tile_mean_var(t):
            u, i = divmod(t, GROUP_TILES)
            if i == 0:
                mean_var_u = stat_pool.tile([P, GROUP_TILES, 2], F32, name="mean_var")
                mean_var[u] = mean_var_u
            nc.vector.bn_aggr(out=mean_var[u][:, i, :], in_=halves[t][:])

        def tile_centre_and_gain(t):
            u, i = divmod(t, GROUP_TILES)
            y_t = y_pool.tile([P, Q], F32, name="y")
            nc.vector.scalar_tensor_tensor(
                out=y_t[:], in0=sup[t][:], scalar=mean_var[u][:, i, 0:1], in1=gain,
                op0=ALU.subtract, op1=ALU.mult,
            )
            y[t] = y_t

        def unit_rstd(u):
            rstd_u = stat_pool.tile([P, GROUP_TILES], F32, name="rstd")
            nc.scalar.activation(
                out=rstd_u[:], in_=mean_var[u][:, :, 1], func=ACT.Abs_reciprocal_sqrt,
                bias=eps[:, 0:1], scale=1.0,
            )
            rstd[u] = rstd_u

        def tile_finish(t):
            u, i = divmod(t, GROUP_TILES)
            g, s = divmod(u, STATES)
            if u < UNITS - 1:
                nc.scalar.activation(
                    out=y[t][:], in_=y[t][:], func=ACT.Copy, scale=rstd[u][:, i : i + 1]
                )
                nc.gpsimd.tensor_tensor(out=y[t][:], in0=y[t][:], in1=shift, op=ALU.add)
            else:
                nc.vector.scalar_tensor_tensor(
                    out=y[t][:], in0=y[t][:], scalar=rstd[u][:, i : i + 1], in1=shift,
                    op0=ALU.mult, op1=ALU.add,
                )
            nc.sync.dma_start(out=out_view[:, g * GROUP_TILES + i, s, :], in_=y[t][:])

        for t in range(-2 * GROUP_TILES, TILES + LAG):
            u, i = divmod(t, GROUP_TILES)
            ahead = u + 2
            if i == LAG and 0 <= u < UNITS:
                unit_rstd(u)
            if ahead < UNITS:
                slice_products(ahead, i)
            g_next = ahead // STATES + 1
            pair = ahead % STATES - 1
            if g_next < GROUPS and pair >= 0:
                if i == 0:
                    x_transposes(g_next, pair)
                if i == 1:
                    x_regroup(g_next, pair)
                if i == 3 and pair == 1:
                    x_quantise(g_next)
            if ahead < UNITS:
                slice_mix(ahead, i)
            if 0 <= t + 1 < TILES:
                tile_halves(t + 1)
            if 0 <= t < TILES:
                tile_centre_and_gain(t)
            if 0 <= t + 1 < TILES:
                tile_mean_var(t + 1)
            if 0 <= t + GROUP_TILES < TILES:
                tile_transposes(t + GROUP_TILES)
            if 0 <= t - LAG:
                tile_finish(t - LAG)
